import numpy as np
import ml_dtypes

BF16 = ml_dtypes.bfloat16


def bf(x):
    return np.asarray(x, np.float32).astype(BF16)


def f32(x):
    return np.asarray(x, np.float32)


def f64(x):
    return np.asarray(x).astype(np.float64)


def striped(idx):
    return np.tile(idx.reshape(-1, 16).T, (8, 1))


V, D, Q, MEM, T, N = 4096, 128, 128, 512, 4, 2048


def setup_inputs():
    return {"table": bf(0.1 * np.random.standard_normal((D, V))), "queries": bf(np.random.standard_normal((D, Q))), "offs": striped(np.random.permutation(np.tile(np.arange(V), 2))[:N])}


def reference(table, queries, offs):
    idx = offs[:16].T.reshape(-1)
    bag = f64(table)[:, idx].reshape(D, T, MEM).sum(axis=1)
    return f64(queries).T @ bag

@@ -1,0 +1,35 @@
+import concourse.mybir as mybir
+
+FEATURES = 128
+VOCAB = 4096
+QUERIES = 128
+SLOTS = 512
+WORDS = 4
+LIST_COLUMNS = SLOTS // 16
+
+FLOPS = 2 * FEATURES * QUERIES * SLOTS * WORDS
+
+BF16, F32, U16 = mybir.dt.bfloat16, mybir.dt.float32, mybir.dt.uint16
+
+
+def tile_decoderrkbmemnn_kernel(tc, table, queries, offs, out):
+    nc = tc.nc
+    with (
+        tc.tile_pool(name="held", bufs=1) as held,
+        tc.psum_pool(name="psum", bufs=1) as psum,
+    ):
+        offsets = held.tile([128, WORDS * LIST_COLUMNS], U16, name="offsets")
+        nc.sync.dma_start(offsets[:], offs)
+        queries_sb = held.tile([FEATURES, QUERIES], BF16, name="queries_sb")
+        nc.sync.dma_start(queries_sb[:], queries)
+        table_sb = held.tile([FEATURES, VOCAB], BF16, name="table_sb")
+        nc.sync.dma_start(table_sb[:], table)
+
+        logits = psum.tile([QUERIES, SLOTS], F32, name="logits")
+        for t in range(WORDS):
+            word_t = table_sb[:].indirect(offsets[:, t * LIST_COLUMNS : (t + 1) * LIST_COLUMNS])
+            nc.tensor.matmul(logits[:], queries_sb[:], word_t, start=(t == 0), stop=(t == WORDS - 1))
+
+        logits_sb = held.tile([QUERIES, SLOTS], F32, name="logits_sb")
+        nc.vector.tensor_copy(logits_sb[:], logits[:])
+        nc.sync.dma_start(out, logits_sb[:])

@@ -5,6 +5,7 @@ VOCAB = 4096
 QUERIES = 128
 SLOTS = 512
 WORDS = 4
+HALF = SLOTS // 2
 LIST_COLUMNS = SLOTS // 16
 
 FLOPS = 2 * FEATURES * QUERIES * SLOTS * WORDS
@@ -25,11 +26,20 @@ def tile_decoderrkbmemnn_kernel(tc, table, queries, offs, out):
         table_sb = held.tile([FEATURES, VOCAB], BF16, name="table_sb")
         nc.sync.dma_start(table_sb[:], table)
 
-        logits = psum.tile([QUERIES, SLOTS], F32, name="logits")
-        for t in range(WORDS):
+        first_words = psum.tile([QUERIES, SLOTS], F32, name="first_words")
+        for t in range(WORDS - 1):
             word_t = table_sb[:].indirect(offsets[:, t * LIST_COLUMNS : (t + 1) * LIST_COLUMNS])
-            nc.tensor.matmul(logits[:], queries_sb[:], word_t, start=(t == 0), stop=(t == WORDS - 1))
+            nc.tensor.matmul(first_words[:], queries_sb[:], word_t, start=(t == 0), stop=(t == WORDS - 2))
 
-        logits_sb = held.tile([QUERIES, SLOTS], F32, name="logits_sb")
-        nc.vector.tensor_copy(logits_sb[:], logits[:])
-        nc.sync.dma_start(out, logits_sb[:])
+        for h in range(2):
+            slots = slice(h * HALF, (h + 1) * HALF)
+            first_column = (WORDS - 1) * LIST_COLUMNS + h * (HALF // 16)
+            last_word = psum.tile([QUERIES, HALF], F32, name=f"last_word{h}")
+            looked_up = table_sb[:].indirect(offsets[:, first_column : first_column + HALF // 16])
+            nc.tensor.matmul(last_word[:], queries_sb[:], looked_up, start=True, stop=True)
+
+            first_sb = held.tile([QUERIES, HALF], F32, name=f"first_sb{h}")
+            nc.scalar.copy(first_sb[:], first_words[:, slots])
+            logits_sb = held.tile([QUERIES, HALF], F32, name=f"logits_sb{h}")
+            nc.vector.tensor_tensor(logits_sb[:], last_word[:], first_sb[:], mybir.AluOpType.add)
+            nc.sync.dma_start(out[:, slots], logits_sb[:])

@@ -5,7 +5,8 @@ VOCAB = 4096
 QUERIES = 128
 SLOTS = 512
 WORDS = 4
-HALF = SLOTS // 2
+PIECES = 4
+PIECE = SLOTS // PIECES
 LIST_COLUMNS = SLOTS // 16
 
 FLOPS = 2 * FEATURES * QUERIES * SLOTS * WORDS
@@ -31,15 +32,15 @@ def tile_decoderrkbmemnn_kernel(tc, table, queries, offs, out):
             word_t = table_sb[:].indirect(offsets[:, t * LIST_COLUMNS : (t + 1) * LIST_COLUMNS])
             nc.tensor.matmul(first_words[:], queries_sb[:], word_t, start=(t == 0), stop=(t == WORDS - 2))
 
-        for h in range(2):
-            slots = slice(h * HALF, (h + 1) * HALF)
-            first_column = (WORDS - 1) * LIST_COLUMNS + h * (HALF // 16)
-            last_word = psum.tile([QUERIES, HALF], F32, name=f"last_word{h}")
-            looked_up = table_sb[:].indirect(offsets[:, first_column : first_column + HALF // 16])
+        for h in range(PIECES):
+            slots = slice(h * PIECE, (h + 1) * PIECE)
+            first_column = (WORDS - 1) * LIST_COLUMNS + h * (PIECE // 16)
+            last_word = psum.tile([QUERIES, PIECE], F32, name=f"last_word{h}")
+            looked_up = table_sb[:].indirect(offsets[:, first_column : first_column + PIECE // 16])
             nc.tensor.matmul(last_word[:], queries_sb[:], looked_up, start=True, stop=True)
 
-            first_sb = held.tile([QUERIES, HALF], F32, name=f"first_sb{h}")
+            first_sb = held.tile([QUERIES, PIECE], F32, name=f"first_sb{h}")
             nc.scalar.copy(first_sb[:], first_words[:, slots])
-            logits_sb = held.tile([QUERIES, HALF], F32, name=f"logits_sb{h}")
+            logits_sb = held.tile([QUERIES, PIECE], F32, name=f"logits_sb{h}")
             nc.vector.tensor_tensor(logits_sb[:], last_word[:], first_sb[:], mybir.AluOpType.add)
             nc.sync.dma_start(out[:, slots], logits_sb[:])

@@ -32,6 +32,8 @@ def tile_decoderrkbmemnn_kernel(tc, table, queries, offs, out):
             word_t = table_sb[:].indirect(offsets[:, t * LIST_COLUMNS : (t + 1) * LIST_COLUMNS])
             nc.tensor.matmul(first_words[:], queries_sb[:], word_t, start=(t == 0), stop=(t == WORDS - 2))
 
+        logits_sb = held.tile([QUERIES, SLOTS], F32, name="logits_sb")
+        stored = 0
         for h in range(PIECES):
             slots = slice(h * PIECE, (h + 1) * PIECE)
             first_column = (WORDS - 1) * LIST_COLUMNS + h * (PIECE // 16)
@@ -41,6 +43,7 @@ def tile_decoderrkbmemnn_kernel(tc, table, queries, offs, out):
 
             first_sb = held.tile([QUERIES, PIECE], F32, name=f"first_sb{h}")
             nc.scalar.copy(first_sb[:], first_words[:, slots])
-            logits_sb = held.tile([QUERIES, PIECE], F32, name=f"logits_sb{h}")
-            nc.vector.tensor_tensor(logits_sb[:], last_word[:], first_sb[:], mybir.AluOpType.add)
-            nc.sync.dma_start(out[:, slots], logits_sb[:])
+            nc.vector.tensor_tensor(logits_sb[:, slots], last_word[:], first_sb[:], mybir.AluOpType.add)
+            if h != PIECES - 2:
+                nc.sync.dma_start(out[:, stored : slots.stop], logits_sb[:, stored : slots.stop])
+                stored = slots.stop

@@ -5,8 +5,7 @@ VOCAB = 4096
 QUERIES = 128
 SLOTS = 512
 WORDS = 4
-PIECES = 4
-PIECE = SLOTS // PIECES
+CUTS = (0, SLOTS // 4, SLOTS // 2, SLOTS)
 LIST_COLUMNS = SLOTS // 16
 
 FLOPS = 2 * FEATURES * QUERIES * SLOTS * WORDS
@@ -32,18 +31,15 @@ def tile_decoderrkbmemnn_kernel(tc, table, queries, offs, out):
             word_t = table_sb[:].indirect(offsets[:, t * LIST_COLUMNS : (t + 1) * LIST_COLUMNS])
             nc.tensor.matmul(first_words[:], queries_sb[:], word_t, start=(t == 0), stop=(t == WORDS - 2))
 
-        logits_sb = held.tile([QUERIES, SLOTS], F32, name="logits_sb")
-        stored = 0
-        for h in range(PIECES):
-            slots = slice(h * PIECE, (h + 1) * PIECE)
-            first_column = (WORDS - 1) * LIST_COLUMNS + h * (PIECE // 16)
-            last_word = psum.tile([QUERIES, PIECE], F32, name=f"last_word{h}")
-            looked_up = table_sb[:].indirect(offsets[:, first_column : first_column + PIECE // 16])
+        for h, (begin, end) in enumerate(zip(CUTS[:-1], CUTS[1:])):
+            first_entry = (WORDS - 1) * SLOTS + begin
+            last_entry = (WORDS - 1) * SLOTS + end
+            last_word = psum.tile([QUERIES, end - begin], F32, name=f"last_word{h}")
+            looked_up = table_sb[:].indirect(offsets[:, first_entry // 16 : last_entry // 16])
             nc.tensor.matmul(last_word[:], queries_sb[:], looked_up, start=True, stop=True)
 
-            first_sb = held.tile([QUERIES, PIECE], F32, name=f"first_sb{h}")
-            nc.scalar.copy(first_sb[:], first_words[:, slots])
-            nc.vector.tensor_tensor(logits_sb[:, slots], last_word[:], first_sb[:], mybir.AluOpType.add)
-            if h != PIECES - 2:
-                nc.sync.dma_start(out[:, stored : slots.stop], logits_sb[:, stored : slots.stop])
-                stored = slots.stop
+            first_sb = held.tile([QUERIES, end - begin], F32, name=f"first_sb{h}")
+            nc.scalar.copy(first_sb[:], first_words[:, begin:end])
+            logits_sb = held.tile([QUERIES, end - begin], F32, name=f"logits_sb{h}")
+            nc.vector.tensor_tensor(logits_sb[:], last_word[:], first_sb[:], mybir.AluOpType.add)
+            nc.sync.dma_start(out[:, begin:end], logits_sb[:])

import concourse.mybir as mybir

FEATURES = 128
VOCAB = 4096
QUERIES = 128
SLOTS = 512
WORDS = 4
CUTS = (0, SLOTS // 4, SLOTS // 2, SLOTS)
LIST_COLUMNS = SLOTS // 16

FLOPS = 2 * FEATURES * QUERIES * SLOTS * WORDS

BF16, F32, U16 = mybir.dt.bfloat16, mybir.dt.float32, mybir.dt.uint16


def tile_decoderrkbmemnn_kernel(tc, table, queries, offs, out):
    nc = tc.nc
    with (
        tc.tile_pool(name="held", bufs=1) as held,
        tc.psum_pool(name="psum", bufs=1) as psum,
    ):
        offsets = held.tile([128, WORDS * LIST_COLUMNS], U16, name="offsets")
        nc.sync.dma_start(offsets[:], offs)
        queries_sb = held.tile([FEATURES, QUERIES], BF16, name="queries_sb")
        nc.sync.dma_start(queries_sb[:], queries)
        table_sb = held.tile([FEATURES, VOCAB], BF16, name="table_sb")
        nc.sync.dma_start(table_sb[:], table)

        first_words = psum.tile([QUERIES, SLOTS], F32, name="first_words")
        for t in range(WORDS - 1):
            word_t = table_sb[:].indirect(offsets[:, t * LIST_COLUMNS : (t + 1) * LIST_COLUMNS])
            nc.tensor.matmul(first_words[:], queries_sb[:], word_t, start=(t == 0), stop=(t == WORDS - 2))

        for h, (begin, end) in enumerate(zip(CUTS[:-1], CUTS[1:])):
            first_entry = (WORDS - 1) * SLOTS + begin
            last_entry = (WORDS - 1) * SLOTS + end
            last_word = psum.tile([QUERIES, end - begin], F32, name=f"last_word{h}")
            looked_up = table_sb[:].indirect(offsets[:, first_entry // 16 : last_entry // 16])
            nc.tensor.matmul(last_word[:], queries_sb[:], looked_up, start=True, stop=True)

            first_sb = held.tile([QUERIES, end - begin], F32, name=f"first_sb{h}")
            nc.scalar.copy(first_sb[:], first_words[:, begin:end])
            logits_sb = held.tile([QUERIES, end - begin], F32, name=f"logits_sb{h}")
            nc.vector.tensor_tensor(logits_sb[:], last_word[:], first_sb[:], mybir.AluOpType.add)
            nc.sync.dma_start(out[:, begin:end], logits_sb[:])
